import numpy as np
import ml_dtypes

BF16 = ml_dtypes.bfloat16


def bf(x):
    return np.asarray(x, np.float32).astype(BF16)


def f32(x):
    return np.asarray(x, np.float32)


def f64(x):
    return np.asarray(x).astype(np.float64)


def striped(idx):
    return np.tile(idx.reshape(-1, 16).T, (8, 1))


C, M, S, N = 512, 1024, 4096, 2048
EPS = 1e-5


def silu(v):
    return v / (1.0 + np.exp(-v))


def setup_inputs():
    return {
        "base": f32(np.random.standard_normal((C, S))),
        "x": f32(np.random.standard_normal((C, N))),
        "gain_h": f32(1.0 + 0.1 * np.random.standard_normal((C, 1))),
        "w_gate": bf(np.random.standard_normal((C, M)) / np.sqrt(C)),
        "w_up": bf(np.random.standard_normal((C, M)) / np.sqrt(C)),
        "w_down": bf(np.random.standard_normal((M, C)) / np.sqrt(M)),
        "gain_f": f32(1.0 + 0.1 * np.random.standard_normal((C, 1))),
        "offs": striped(np.random.permutation(S)[:N]),
    }


def reference(base, x, gain_h, w_gate, w_up, w_down, gain_f, offs):
    idx = offs[:16].T.reshape(-1)
    x = f64(x)
    h = x * f64(gain_h) / np.sqrt(np.mean(x * x, axis=0, keepdims=True) + EPS)
    a = silu(f64(w_gate).T @ h) * (f64(w_up).T @ h)
    y = x + f64(w_down).T @ a
    r = 1.0 / np.sqrt(np.mean(y * y, axis=0, keepdims=True) + EPS)
    out = f64(base).copy()
    out[:, idx] = (y * f64(gain_f)) * r
    return out

@@ -1,0 +1,121 @@
+import concourse.mybir as mybir
+
+F32 = mybir.dt.float32
+BF16 = mybir.dt.bfloat16
+U16 = mybir.dt.uint16
+MULT = mybir.AluOpType.mult
+ADD = mybir.AluOpType.add
+ACT = mybir.ActivationFunctionType
+
+P = 128
+C, M, S, N = 512, 1024, 4096, 2048
+EPS = 1e-5
+CB = C // P
+MB = M // P
+CHUNK = 512
+PIECE = 1024
+CHUNKS = N // CHUNK
+CHUNKS_PER_PIECE = PIECE // CHUNK
+
+FLOPS = 2 * N * 3 * C * M
+
+
+def tile_metajanusrrpram_b_kernel(tc, base, x, gain_h, w_gate, w_up, w_down, gain_f, offs, out):
+    nc = tc.nc
+    with (
+        tc.tile_pool(name="held", bufs=1) as held,
+        tc.tile_pool(name="work", bufs=2) as work,
+        tc.psum_pool(name="banks", bufs=8) as banks,
+    ):
+        offsets = held.tile([P, N // 16], U16, name="offsets")
+        nc.sync.dma_start(offsets[:], offs)
+
+        x_blocks = x.rearrange("(b p) n -> p b n", p=P)
+        x_sb = [held.tile([P, CB, CHUNK], F32, name=f"x{t}") for t in range(CHUNKS)]
+        nc.sync.dma_start(x_sb[0][:], x_blocks[:, :, 0:CHUNK])
+
+        gain_h_sb = held.tile([P, CB], F32, name="gain_h_sb")
+        gain_f_sb = held.tile([P, CB], F32, name="gain_f_sb")
+        with nc.allow_non_contiguous_dma(reason="one gain to a partition, 512 elements in all"):
+            nc.sync.dma_start(gain_h_sb[:], gain_h.rearrange("(b p) o -> p (b o)", p=P))
+            nc.sync.dma_start(gain_f_sb[:], gain_f.rearrange("(b p) o -> p (b o)", p=P))
+
+        w_gate_sb = held.tile([P, CB, M], BF16, name="w_gate_sb")
+        w_up_sb = held.tile([P, CB, M], BF16, name="w_up_sb")
+        w_down_sb = held.tile([P, MB, C], BF16, name="w_down_sb")
+        nc.sync.dma_start(w_gate_sb[:], w_gate.rearrange("(b p) m -> p b m", p=P))
+        nc.sync.dma_start(w_up_sb[:], w_up.rearrange("(b p) m -> p b m", p=P))
+        for t in range(1, CHUNKS):
+            nc.sync.dma_start(x_sb[t][:], x_blocks[:, :, t * CHUNK:(t + 1) * CHUNK])
+        nc.sync.dma_start(w_down_sb[:], w_down.rearrange("(b p) c -> p b c", p=P))
+
+        window = [held.tile([P, S], F32, name=f"window{c}") for c in range(CB)]
+        for c in range(CB):
+            nc.sync.dma_start(window[c][:], base[c * P:(c + 1) * P, :])
+
+        mean_w = held.tile([P, P], BF16, name="mean_w")
+        nc.vector.memset(mean_w[:], 1.0 / C)
+        eps = held.tile([P, 1], F32, name="eps")
+        nc.vector.memset(eps[:], EPS)
+
+        def inverse_rms(dest, squares):
+            mean_ps = banks.tile([P, CHUNK], F32, name="mean_ps", tag="bank")
+            for c in range(CB):
+                nc.tensor.matmul(mean_ps[:], mean_w[:], squares[:, c, :], start=(c == 0), stop=(c == CB - 1))
+            nc.scalar.activation(dest, mean_ps[:], ACT.Abs_reciprocal_sqrt, bias=eps[:], scale=1.0)
+
+        h_sb = [held.tile([P, CB, CHUNK], BF16, name=f"h{t}") for t in range(CHUNKS)]
+        for t in range(CHUNKS):
+            x_sq = work.tile([P, CB, CHUNK], BF16, name="x_sq")
+            for c in range(CB):
+                nc.scalar.activation(x_sq[:, c, :], x_sb[t][:, c, :], ACT.Square)
+            x_rinv = work.tile([P, CHUNK], F32, name="x_rinv")
+            inverse_rms(x_rinv[:], x_sq)
+            for c in range(CB):
+                nc.vector.scalar_tensor_tensor(
+                    h_sb[t][:, c, :], x_sb[t][:, c, :], gain_h_sb[:, c:c + 1], x_rinv[:], MULT, MULT
+                )
+
+        for t in range(CHUNKS):
+            piece, part = divmod(t, CHUNKS_PER_PIECE)
+            if part == 0:
+                y_gained = work.tile([P, CB, PIECE], F32, name="y_gained")
+                y_rinv = work.tile([P, PIECE], F32, name="y_rinv")
+            tokens = slice(part * CHUNK, (part + 1) * CHUNK)
+
+            a_sb = work.tile([P, MB, CHUNK], BF16, name="a_sb")
+            for m in range(MB):
+                hidden = slice(m * P, (m + 1) * P)
+                gate_ps = banks.tile([P, CHUNK], F32, name="gate_ps", tag="bank")
+                for c in range(CB):
+                    nc.tensor.matmul(gate_ps[:], w_gate_sb[:, c, hidden], h_sb[t][:, c, :],
+                                     start=(c == 0), stop=(c == CB - 1))
+                up_ps = banks.tile([P, CHUNK], F32, name="up_ps", tag="bank")
+                for c in range(CB):
+                    nc.tensor.matmul(up_ps[:], w_up_sb[:, c, hidden], h_sb[t][:, c, :],
+                                     start=(c == 0), stop=(c == CB - 1))
+                gate_silu = work.tile([P, CHUNK], F32, name="gate_silu")
+                nc.scalar.activation(gate_silu[:], gate_ps[:], ACT.Silu)
+                nc.vector.tensor_tensor(a_sb[:, m, :], gate_silu[:], up_ps[:], MULT)
+
+            y_sb = work.tile([P, CB, CHUNK], F32, name="y_sb", bufs=1)
+            y_sq = work.tile([P, CB, CHUNK], BF16, name="y_sq", bufs=1)
+            for c in range(CB):
+                channels = slice(c * P, (c + 1) * P)
+                down_ps = banks.tile([P, CHUNK], F32, name="down_ps", tag="bank")
+                for m in range(MB):
+                    nc.tensor.matmul(down_ps[:], w_down_sb[:, m, channels], a_sb[:, m, :],
+                                     start=(m == 0), stop=(m == MB - 1))
+                nc.vector.tensor_tensor(y_sb[:, c, :], down_ps[:], x_sb[t][:, c, :], ADD)
+                nc.scalar.activation(y_sq[:, c, :], y_sb[:, c, :], ACT.Square)
+                nc.scalar.activation(y_gained[:, c, tokens], y_sb[:, c, :], ACT.Identity,
+                                     scale=gain_f_sb[:, c:c + 1])
+            inverse_rms(y_rinv[:, tokens], y_sq)
+
+            if part == CHUNKS_PER_PIECE - 1:
+                piece_offsets = offsets[:, piece * (PIECE // 16):(piece + 1) * (PIECE // 16)]
+                for c in range(CB):
+                    nc.vector.tensor_tensor(window[c][:].indirect(piece_offsets), y_gained[:, c, :], y_rinv[:], MULT)
+
+        for c in range(CB):
+            nc.sync.dma_start(out[c * P:(c + 1) * P, :], window[c][:])

@@ -16,6 +16,7 @@ CHUNK = 512
 PIECE = 1024
 CHUNKS = N // CHUNK
 CHUNKS_PER_PIECE = PIECE // CHUNK
+PIECES = N // PIECE
 
 FLOPS = 2 * N * 3 * C * M
 
@@ -25,14 +26,15 @@ def tile_metajanusrrpram_b_kernel(tc, base, x, gain_h, w_gate, w_up, w_down, gai
     with (
         tc.tile_pool(name="held", bufs=1) as held,
         tc.tile_pool(name="work", bufs=2) as work,
+        tc.tile_pool(name="evacuated", bufs=5) as evacuated,
         tc.psum_pool(name="banks", bufs=8) as banks,
     ):
         offsets = held.tile([P, N // 16], U16, name="offsets")
         nc.sync.dma_start(offsets[:], offs)
 
         x_blocks = x.rearrange("(b p) n -> p b n", p=P)
-        x_sb = [held.tile([P, CB, CHUNK], F32, name=f"x{t}") for t in range(CHUNKS)]
-        nc.sync.dma_start(x_sb[0][:], x_blocks[:, :, 0:CHUNK])
+        resid = [held.tile([P, CB, CHUNK], F32, name=f"resid{t}") for t in range(CHUNKS)]
+        nc.sync.dma_start(resid[0][:], x_blocks[:, :, 0:CHUNK])
 
         gain_h_sb = held.tile([P, CB], F32, name="gain_h_sb")
         gain_f_sb = held.tile([P, CB], F32, name="gain_f_sb")
@@ -46,7 +48,7 @@ def tile_metajanusrrpram_b_kernel(tc, base, x, gain_h, w_gate, w_up, w_down, gai
         nc.sync.dma_start(w_gate_sb[:], w_gate.rearrange("(b p) m -> p b m", p=P))
         nc.sync.dma_start(w_up_sb[:], w_up.rearrange("(b p) m -> p b m", p=P))
         for t in range(1, CHUNKS):
-            nc.sync.dma_start(x_sb[t][:], x_blocks[:, :, t * CHUNK:(t + 1) * CHUNK])
+            nc.sync.dma_start(resid[t][:], x_blocks[:, :, t * CHUNK:(t + 1) * CHUNK])
         nc.sync.dma_start(w_down_sb[:], w_down.rearrange("(b p) c -> p b c", p=P))
 
         window = [held.tile([P, S], F32, name=f"window{c}") for c in range(CB)]
@@ -58,64 +60,80 @@ def tile_metajanusrrpram_b_kernel(tc, base, x, gain_h, w_gate, w_up, w_down, gai
         eps = held.tile([P, 1], F32, name="eps")
         nc.vector.memset(eps[:], EPS)
 
-        def inverse_rms(dest, squares):
+        def mean_of_squares(values):
+            squares = work.tile([P, CB, CHUNK], BF16, name="squares")
+            for c in range(CB):
+                if c % 2 == 0:
+                    nc.scalar.activation(squares[:, c, :], values[:, c, :], ACT.Square)
+                else:
+                    nc.vector.tensor_tensor(squares[:, c, :], values[:, c, :], values[:, c, :], MULT)
             mean_ps = banks.tile([P, CHUNK], F32, name="mean_ps", tag="bank")
             for c in range(CB):
                 nc.tensor.matmul(mean_ps[:], mean_w[:], squares[:, c, :], start=(c == 0), stop=(c == CB - 1))
-            nc.scalar.activation(dest, mean_ps[:], ACT.Abs_reciprocal_sqrt, bias=eps[:], scale=1.0)
+            return mean_ps
 
         h_sb = [held.tile([P, CB, CHUNK], BF16, name=f"h{t}") for t in range(CHUNKS)]
-        for t in range(CHUNKS):
-            x_sq = work.tile([P, CB, CHUNK], BF16, name="x_sq")
-            for c in range(CB):
-                nc.scalar.activation(x_sq[:, c, :], x_sb[t][:, c, :], ACT.Square)
-            x_rinv = work.tile([P, CHUNK], F32, name="x_rinv")
-            inverse_rms(x_rinv[:], x_sq)
-            for c in range(CB):
-                nc.vector.scalar_tensor_tensor(
-                    h_sb[t][:, c, :], x_sb[t][:, c, :], gain_h_sb[:, c:c + 1], x_rinv[:], MULT, MULT
-                )
-
-        for t in range(CHUNKS):
-            piece, part = divmod(t, CHUNKS_PER_PIECE)
-            if part == 0:
-                y_gained = work.tile([P, CB, PIECE], F32, name="y_gained")
-                y_rinv = work.tile([P, PIECE], F32, name="y_rinv")
-            tokens = slice(part * CHUNK, (part + 1) * CHUNK)
-
-            a_sb = work.tile([P, MB, CHUNK], BF16, name="a_sb")
-            for m in range(MB):
-                hidden = slice(m * P, (m + 1) * P)
-                gate_ps = banks.tile([P, CHUNK], F32, name="gate_ps", tag="bank")
+        for first, count in ((0, 1), (1, CHUNKS - 1)):
+            x_mean = held.tile([P, count * CHUNK], F32, name=f"x_mean{first}")
+            x_rinv = held.tile([P, count * CHUNK], F32, name=f"x_rinv{first}")
+            for k in range(count):
+                nc.vector.tensor_copy(x_mean[:, k * CHUNK:(k + 1) * CHUNK], mean_of_squares(resid[first + k])[:])
+            nc.scalar.activation(x_rinv[:], x_mean[:], ACT.Abs_reciprocal_sqrt, bias=eps[:], scale=1.0)
+            for k in range(count):
                 for c in range(CB):
-                    nc.tensor.matmul(gate_ps[:], w_gate_sb[:, c, hidden], h_sb[t][:, c, :],
-                                     start=(c == 0), stop=(c == CB - 1))
-                up_ps = banks.tile([P, CHUNK], F32, name="up_ps", tag="bank")
-                for c in range(CB):
-                    nc.tensor.matmul(up_ps[:], w_up_sb[:, c, hidden], h_sb[t][:, c, :],
-                                     start=(c == 0), stop=(c == CB - 1))
-                gate_silu = work.tile([P, CHUNK], F32, name="gate_silu")
-                nc.scalar.activation(gate_silu[:], gate_ps[:], ACT.Silu)
-                nc.vector.tensor_tensor(a_sb[:, m, :], gate_silu[:], up_ps[:], MULT)
+                    nc.vector.scalar_tensor_tensor(
+                        h_sb[first + k][:, c, :], resid[first + k][:, c, :], gain_h_sb[:, c:c + 1],
+                        x_rinv[:, k * CHUNK:(k + 1) * CHUNK], MULT, MULT,
+                    )
 
-            y_sb = work.tile([P, CB, CHUNK], F32, name="y_sb", bufs=1)
-            y_sq = work.tile([P, CB, CHUNK], BF16, name="y_sq", bufs=1)
+        def place(piece, y_gained, y_rinv):
+            piece_offsets = offsets[:, piece * (PIECE // 16):(piece + 1) * (PIECE // 16)]
             for c in range(CB):
-                channels = slice(c * P, (c + 1) * P)
-                down_ps = banks.tile([P, CHUNK], F32, name="down_ps", tag="bank")
+                nc.vector.tensor_tensor(window[c][:].indirect(piece_offsets), y_gained[:, c, :], y_rinv[:], MULT)
+
+        waiting = None
+        for piece in range(PIECES):
+            chunks = range(piece * CHUNKS_PER_PIECE, (piece + 1) * CHUNKS_PER_PIECE)
+
+            a_sb = {}
+            for t in chunks:
+                a_sb[t] = work.tile([P, MB, CHUNK], BF16, name="a_sb")
                 for m in range(MB):
-                    nc.tensor.matmul(down_ps[:], w_down_sb[:, m, channels], a_sb[:, m, :],
-                                     start=(m == 0), stop=(m == MB - 1))
-                nc.vector.tensor_tensor(y_sb[:, c, :], down_ps[:], x_sb[t][:, c, :], ADD)
-                nc.scalar.activation(y_sq[:, c, :], y_sb[:, c, :], ACT.Square)
-                nc.scalar.activation(y_gained[:, c, tokens], y_sb[:, c, :], ACT.Identity,
-                                     scale=gain_f_sb[:, c:c + 1])
-            inverse_rms(y_rinv[:, tokens], y_sq)
+                    hidden = slice(m * P, (m + 1) * P)
+                    gate_ps = banks.tile([P, CHUNK], F32, name="gate_ps", tag="bank")
+                    for c in range(CB):
+                        nc.tensor.matmul(gate_ps[:], w_gate_sb[:, c, hidden], h_sb[t][:, c, :],
+                                         start=(c == 0), stop=(c == CB - 1))
+                    up_ps = banks.tile([P, CHUNK], F32, name="up_ps", tag="bank")
+                    for c in range(CB):
+                        nc.tensor.matmul(up_ps[:], w_up_sb[:, c, hidden], h_sb[t][:, c, :],
+                                         start=(c == 0), stop=(c == CB - 1))
+                    gate_silu = evacuated.tile([P, CHUNK], F32, name="gate_silu")
+                    nc.scalar.activation(gate_silu[:], gate_ps[:], ACT.Silu)
+                    up_sb = evacuated.tile([P, CHUNK], F32, name="up_sb")
+                    nc.scalar.activation(up_sb[:], up_ps[:], ACT.Copy)
+                    nc.vector.tensor_tensor(a_sb[t][:, m, :], gate_silu[:], up_sb[:], MULT)
 
-            if part == CHUNKS_PER_PIECE - 1:
-                piece_offsets = offsets[:, piece * (PIECE // 16):(piece + 1) * (PIECE // 16)]
+            if waiting is not None:
+                place(*waiting)
+
+            y_gained = work.tile([P, CB, PIECE], F32, name="y_gained")
+            y_rinv = work.tile([P, PIECE], F32, name="y_rinv")
+            for t in chunks:
+                tokens = slice((t - chunks[0]) * CHUNK, (t - chunks[0] + 1) * CHUNK)
                 for c in range(CB):
-                    nc.vector.tensor_tensor(window[c][:].indirect(piece_offsets), y_gained[:, c, :], y_rinv[:], MULT)
+                    channels = slice(c * P, (c + 1) * P)
+                    down_ps = banks.tile([P, CHUNK], F32, name="down_ps", tag="bank")
+                    for m in range(MB):
+                        nc.tensor.matmul(down_ps[:], w_down_sb[:, m, channels], a_sb[t][:, m, :],
+                                         start=(m == 0), stop=(m == MB - 1))
+                    nc.vector.tensor_tensor(resid[t][:, c, :], down_ps[:], resid[t][:, c, :], ADD)
+                    nc.scalar.activation(y_gained[:, c, tokens], resid[t][:, c, :], ACT.Identity,
+                                         scale=gain_f_sb[:, c:c + 1])
+                nc.scalar.activation(y_rinv[:, tokens], mean_of_squares(resid[t])[:], ACT.Abs_reciprocal_sqrt,
+                                     bias=eps[:], scale=1.0)
+            waiting = (piece, y_gained, y_rinv)
 
+        place(*waiting)
         for c in range(CB):
             nc.sync.dma_start(out[c * P:(c + 1) * P, :], window[c][:])

@@ -26,7 +26,7 @@ def tile_metajanusrrpram_b_kernel(tc, base, x, gain_h, w_gate, w_up, w_down, gai
     with (
         tc.tile_pool(name="held", bufs=1) as held,
         tc.tile_pool(name="work", bufs=2) as work,
-        tc.tile_pool(name="evacuated", bufs=5) as evacuated,
+        tc.tile_pool(name="evacuated", bufs=8) as evacuated,
         tc.psum_pool(name="banks", bufs=8) as banks,
     ):
         offsets = held.tile([P, N // 16], U16, name="offsets")
@@ -72,26 +72,32 @@ def tile_metajanusrrpram_b_kernel(tc, base, x, gain_h, w_gate, w_up, w_down, gai
                 nc.tensor.matmul(mean_ps[:], mean_w[:], squares[:, c, :], start=(c == 0), stop=(c == CB - 1))
             return mean_ps
 
+        x_rinv = held.tile([P, N], F32, name="x_rinv")
+        nc.scalar.activation(x_rinv[:, 0:CHUNK], mean_of_squares(resid[0])[:], ACT.Abs_reciprocal_sqrt,
+                             bias=eps[:], scale=1.0)
+        x_mean = held.tile([P, N - CHUNK], F32, name="x_mean")
+        for t in range(1, CHUNKS):
+            nc.vector.tensor_copy(x_mean[:, (t - 1) * CHUNK:t * CHUNK], mean_of_squares(resid[t])[:])
+        nc.scalar.activation(x_rinv[:, CHUNK:N], x_mean[:], ACT.Abs_reciprocal_sqrt, bias=eps[:], scale=1.0)
         h_sb = [held.tile([P, CB, CHUNK], BF16, name=f"h{t}") for t in range(CHUNKS)]
-        for first, count in ((0, 1), (1, CHUNKS - 1)):
-            x_mean = held.tile([P, count * CHUNK], F32, name=f"x_mean{first}")
-            x_rinv = held.tile([P, count * CHUNK], F32, name=f"x_rinv{first}")
-            for k in range(count):
-                nc.vector.tensor_copy(x_mean[:, k * CHUNK:(k + 1) * CHUNK], mean_of_squares(resid[first + k])[:])
-            nc.scalar.activation(x_rinv[:], x_mean[:], ACT.Abs_reciprocal_sqrt, bias=eps[:], scale=1.0)
-            for k in range(count):
-                for c in range(CB):
-                    nc.vector.scalar_tensor_tensor(
-                        h_sb[first + k][:, c, :], resid[first + k][:, c, :], gain_h_sb[:, c:c + 1],
-                        x_rinv[:, k * CHUNK:(k + 1) * CHUNK], MULT, MULT,
-                    )
+        for t in range(CHUNKS):
+            for c in range(CB):
+                nc.vector.scalar_tensor_tensor(
+                    h_sb[t][:, c, :], resid[t][:, c, :], gain_h_sb[:, c:c + 1],
+                    x_rinv[:, t * CHUNK:(t + 1) * CHUNK], MULT, MULT,
+                )
 
-        def place(piece, y_gained, y_rinv):
+        def place(piece, y_rinv):
             piece_offsets = offsets[:, piece * (PIECE // 16):(piece + 1) * (PIECE // 16)]
             for c in range(CB):
-                nc.vector.tensor_tensor(window[c][:].indirect(piece_offsets), y_gained[:, c, :], y_rinv[:], MULT)
+                y_gained = work.tile([P, PIECE], F32, name="y_gained", bufs=CB)
+                for k in range(CHUNKS_PER_PIECE):
+                    nc.scalar.activation(y_gained[:, k * CHUNK:(k + 1) * CHUNK],
+                                         resid[piece * CHUNKS_PER_PIECE + k][:, c, :], ACT.Identity,
+                                         scale=gain_f_sb[:, c:c + 1])
+                nc.vector.tensor_tensor(window[c][:].indirect(piece_offsets), y_gained[:], y_rinv[:], MULT)
 
-        waiting = None
+        normed = None
         for piece in range(PIECES):
             chunks = range(piece * CHUNKS_PER_PIECE, (piece + 1) * CHUNKS_PER_PIECE)
 
@@ -114,10 +120,9 @@ def tile_metajanusrrpram_b_kernel(tc, base, x, gain_h, w_gate, w_up, w_down, gai
                     nc.scalar.activation(up_sb[:], up_ps[:], ACT.Copy)
                     nc.vector.tensor_tensor(a_sb[t][:, m, :], gate_silu[:], up_sb[:], MULT)
 
-            if waiting is not None:
-                place(*waiting)
+            if normed is not None:
+                place(*normed)
 
-            y_gained = work.tile([P, CB, PIECE], F32, name="y_gained")
             y_rinv = work.tile([P, PIECE], F32, name="y_rinv")
             for t in chunks:
                 tokens = slice((t - chunks[0]) * CHUNK, (t - chunks[0] + 1) * CHUNK)
@@ -128,12 +133,10 @@ def tile_metajanusrrpram_b_kernel(tc, base, x, gain_h, w_gate, w_up, w_down, gai
                         nc.tensor.matmul(down_ps[:], w_down_sb[:, m, channels], a_sb[t][:, m, :],
                                          start=(m == 0), stop=(m == MB - 1))
                     nc.vector.tensor_tensor(resid[t][:, c, :], down_ps[:], resid[t][:, c, :], ADD)
-                    nc.scalar.activation(y_gained[:, c, tokens], resid[t][:, c, :], ACT.Identity,
-                                         scale=gain_f_sb[:, c:c + 1])
                 nc.scalar.activation(y_rinv[:, tokens], mean_of_squares(resid[t])[:], ACT.Abs_reciprocal_sqrt,
                                      bias=eps[:], scale=1.0)
-            waiting = (piece, y_gained, y_rinv)
+            normed = (piece, y_rinv)
 
-        place(*waiting)
+        place(*normed)
         for c in range(CB):
             nc.sync.dma_start(out[c * P:(c + 1) * P, :], window[c][:])

@@ -72,20 +72,17 @@ def tile_metajanusrrpram_b_kernel(tc, base, x, gain_h, w_gate, w_up, w_down, gai
                 nc.tensor.matmul(mean_ps[:], mean_w[:], squares[:, c, :], start=(c == 0), stop=(c == CB - 1))
             return mean_ps
 
-        x_rinv = held.tile([P, N], F32, name="x_rinv")
-        nc.scalar.activation(x_rinv[:, 0:CHUNK], mean_of_squares(resid[0])[:], ACT.Abs_reciprocal_sqrt,
-                             bias=eps[:], scale=1.0)
-        x_mean = held.tile([P, N - CHUNK], F32, name="x_mean")
-        for t in range(1, CHUNKS):
-            nc.vector.tensor_copy(x_mean[:, (t - 1) * CHUNK:t * CHUNK], mean_of_squares(resid[t])[:])
-        nc.scalar.activation(x_rinv[:, CHUNK:N], x_mean[:], ACT.Abs_reciprocal_sqrt, bias=eps[:], scale=1.0)
         h_sb = [held.tile([P, CB, CHUNK], BF16, name=f"h{t}") for t in range(CHUNKS)]
-        for t in range(CHUNKS):
-            for c in range(CB):
-                nc.vector.scalar_tensor_tensor(
-                    h_sb[t][:, c, :], resid[t][:, c, :], gain_h_sb[:, c:c + 1],
-                    x_rinv[:, t * CHUNK:(t + 1) * CHUNK], MULT, MULT,
-                )
+
+        def first_norm(piece):
+            for t in range(piece * CHUNKS_PER_PIECE, (piece + 1) * CHUNKS_PER_PIECE):
+                x_rinv = work.tile([P, CHUNK], F32, name="x_rinv")
+                nc.scalar.activation(x_rinv[:], mean_of_squares(resid[t])[:], ACT.Abs_reciprocal_sqrt,
+                                     bias=eps[:], scale=1.0)
+                for c in range(CB):
+                    nc.vector.scalar_tensor_tensor(
+                        h_sb[t][:, c, :], resid[t][:, c, :], gain_h_sb[:, c:c + 1], x_rinv[:], MULT, MULT
+                    )
 
         def place(piece, y_rinv):
             piece_offsets = offsets[:, piece * (PIECE // 16):(piece + 1) * (PIECE // 16)]
@@ -97,6 +94,7 @@ def tile_metajanusrrpram_b_kernel(tc, base, x, gain_h, w_gate, w_up, w_down, gai
                                          scale=gain_f_sb[:, c:c + 1])
                 nc.vector.tensor_tensor(window[c][:].indirect(piece_offsets), y_gained[:], y_rinv[:], MULT)
 
+        first_norm(0)
         normed = None
         for piece in range(PIECES):
             chunks = range(piece * CHUNKS_PER_PIECE, (piece + 1) * CHUNKS_PER_PIECE)
@@ -122,6 +120,8 @@ def tile_metajanusrrpram_b_kernel(tc, base, x, gain_h, w_gate, w_up, w_down, gai
 
             if normed is not None:
                 place(*normed)
+            if piece + 1 < PIECES:
+                first_norm(piece + 1)
 
             y_rinv = work.tile([P, PIECE], F32, name="y_rinv")
             for t in chunks:

@@ -13,7 +13,7 @@ EPS = 1e-5
 CB = C // P
 MB = M // P
 CHUNK = 512
-PIECE = 1024
+PIECE = 512
 CHUNKS = N // CHUNK
 CHUNKS_PER_PIECE = PIECE // CHUNK
 PIECES = N // PIECE

@@ -13,10 +13,7 @@ EPS = 1e-5
 CB = C // P
 MB = M // P
 CHUNK = 512
-PIECE = 512
 CHUNKS = N // CHUNK
-CHUNKS_PER_PIECE = PIECE // CHUNK
-PIECES = N // PIECE
 
 FLOPS = 2 * N * 3 * C * M
 
@@ -29,9 +26,6 @@ def tile_metajanusrrpram_b_kernel(tc, base, x, gain_h, w_gate, w_up, w_down, gai
         tc.tile_pool(name="evacuated", bufs=8) as evacuated,
         tc.psum_pool(name="banks", bufs=8) as banks,
     ):
-        offsets = held.tile([P, N // 16], U16, name="offsets")
-        nc.sync.dma_start(offsets[:], offs)
-
         x_blocks = x.rearrange("(b p) n -> p b n", p=P)
         resid = [held.tile([P, CB, CHUNK], F32, name=f"resid{t}") for t in range(CHUNKS)]
         nc.sync.dma_start(resid[0][:], x_blocks[:, :, 0:CHUNK])
@@ -39,17 +33,20 @@ def tile_metajanusrrpram_b_kernel(tc, base, x, gain_h, w_gate, w_up, w_down, gai
         gain_h_sb = held.tile([P, CB], F32, name="gain_h_sb")
         gain_f_sb = held.tile([P, CB], F32, name="gain_f_sb")
         with nc.allow_non_contiguous_dma(reason="one gain to a partition, 512 elements in all"):
-            nc.sync.dma_start(gain_h_sb[:], gain_h.rearrange("(b p) o -> p (b o)", p=P))
-            nc.sync.dma_start(gain_f_sb[:], gain_f.rearrange("(b p) o -> p (b o)", p=P))
+            nc.scalar.dma_start(gain_h_sb[:], gain_h.rearrange("(b p) o -> p (b o)", p=P))
+            nc.scalar.dma_start(gain_f_sb[:], gain_f.rearrange("(b p) o -> p (b o)", p=P))
 
         w_gate_sb = held.tile([P, CB, M], BF16, name="w_gate_sb")
         w_up_sb = held.tile([P, CB, M], BF16, name="w_up_sb")
         w_down_sb = held.tile([P, MB, C], BF16, name="w_down_sb")
         nc.sync.dma_start(w_gate_sb[:], w_gate.rearrange("(b p) m -> p b m", p=P))
         nc.sync.dma_start(w_up_sb[:], w_up.rearrange("(b p) m -> p b m", p=P))
-        for t in range(1, CHUNKS):
-            nc.sync.dma_start(resid[t][:], x_blocks[:, :, t * CHUNK:(t + 1) * CHUNK])
+        nc.sync.dma_start(resid[1][:], x_blocks[:, :, CHUNK:2 * CHUNK])
         nc.sync.dma_start(w_down_sb[:], w_down.rearrange("(b p) c -> p b c", p=P))
+        offsets = held.tile([P, N // 16], U16, name="offsets")
+        nc.sync.dma_start(offsets[:], offs)
+        for t in range(2, CHUNKS):
+            nc.sync.dma_start(resid[t][:], x_blocks[:, :, t * CHUNK:(t + 1) * CHUNK])
 
         window = [held.tile([P, S], F32, name=f"window{c}") for c in range(CB)]
         for c in range(CB):
@@ -60,8 +57,8 @@ def tile_metajanusrrpram_b_kernel(tc, base, x, gain_h, w_gate, w_up, w_down, gai
         eps = held.tile([P, 1], F32, name="eps")
         nc.vector.memset(eps[:], EPS)
 
-        def mean_of_squares(values):
-            squares = work.tile([P, CB, CHUNK], BF16, name="squares")
+        def inverse_rms(values, rinv):
+            squares = work.tile([P, CB, CHUNK], BF16, name="squares", bufs=3)
             for c in range(CB):
                 if c % 2 == 0:
                     nc.scalar.activation(squares[:, c, :], values[:, c, :], ACT.Square)
@@ -70,73 +67,69 @@ def tile_metajanusrrpram_b_kernel(tc, base, x, gain_h, w_gate, w_up, w_down, gai
             mean_ps = banks.tile([P, CHUNK], F32, name="mean_ps", tag="bank")
             for c in range(CB):
                 nc.tensor.matmul(mean_ps[:], mean_w[:], squares[:, c, :], start=(c == 0), stop=(c == CB - 1))
-            return mean_ps
+            nc.scalar.activation(rinv[:], mean_ps[:], ACT.Abs_reciprocal_sqrt, bias=eps[:], scale=1.0)
 
         h_sb = [held.tile([P, CB, CHUNK], BF16, name=f"h{t}") for t in range(CHUNKS)]
 
-        def first_norm(piece):
-            for t in range(piece * CHUNKS_PER_PIECE, (piece + 1) * CHUNKS_PER_PIECE):
-                x_rinv = work.tile([P, CHUNK], F32, name="x_rinv")
-                nc.scalar.activation(x_rinv[:], mean_of_squares(resid[t])[:], ACT.Abs_reciprocal_sqrt,
-                                     bias=eps[:], scale=1.0)
-                for c in range(CB):
-                    nc.vector.scalar_tensor_tensor(
-                        h_sb[t][:, c, :], resid[t][:, c, :], gain_h_sb[:, c:c + 1], x_rinv[:], MULT, MULT
-                    )
-
-        def place(piece, y_rinv):
-            piece_offsets = offsets[:, piece * (PIECE // 16):(piece + 1) * (PIECE // 16)]
+        def first_norm(t):
+            x_rinv = work.tile([P, CHUNK], F32, name="x_rinv")
+            inverse_rms(resid[t], x_rinv)
             for c in range(CB):
-                y_gained = work.tile([P, PIECE], F32, name="y_gained", bufs=CB)
-                for k in range(CHUNKS_PER_PIECE):
-                    nc.scalar.activation(y_gained[:, k * CHUNK:(k + 1) * CHUNK],
-                                         resid[piece * CHUNKS_PER_PIECE + k][:, c, :], ACT.Identity,
-                                         scale=gain_f_sb[:, c:c + 1])
-                nc.vector.tensor_tensor(window[c][:].indirect(piece_offsets), y_gained[:], y_rinv[:], MULT)
+                nc.vector.scalar_tensor_tensor(
+                    h_sb[t][:, c, :], resid[t][:, c, :], gain_h_sb[:, c:c + 1], x_rinv[:], MULT, MULT
+                )
+
+        def gate_up(t):
+            a_sb = work.tile([P, MB, CHUNK], BF16, name="a_sb")
+            for m in range(MB):
+                hidden = slice(m * P, (m + 1) * P)
+                gate_ps = banks.tile([P, CHUNK], F32, name="gate_ps", tag="bank")
+                for c in range(CB):
+                    nc.tensor.matmul(gate_ps[:], w_gate_sb[:, c, hidden], h_sb[t][:, c, :],
+                                     start=(c == 0), stop=(c == CB - 1))
+                up_ps = banks.tile([P, CHUNK], F32, name="up_ps", tag="bank")
+                for c in range(CB):
+                    nc.tensor.matmul(up_ps[:], w_up_sb[:, c, hidden], h_sb[t][:, c, :],
+                                     start=(c == 0), stop=(c == CB - 1))
+                gate_silu = evacuated.tile([P, CHUNK], F32, name="gate_silu")
+                nc.scalar.activation(gate_silu[:], gate_ps[:], ACT.Silu)
+                up_sb = evacuated.tile([P, CHUNK], F32, name="up_sb")
+                nc.scalar.activation(up_sb[:], up_ps[:], ACT.Copy)
+                nc.vector.tensor_tensor(a_sb[:, m, :], gate_silu[:], up_sb[:], MULT)
+            return a_sb
+
+        def down(t, a_sb):
+            for group in ((0, 1), (2,), (3,)):
+                down_ps = {c: banks.tile([P, CHUNK], F32, name="down_ps", tag="bank") for c in group}
+                for m in range(MB):
+                    for c in group:
+                        nc.tensor.matmul(down_ps[c][:], w_down_sb[:, m, c * P:(c + 1) * P], a_sb[:, m, :],
+                                         start=(m == 0), stop=(m == MB - 1))
+                for c in group:
+                    nc.vector.tensor_tensor(resid[t][:, c, :], down_ps[c][:], resid[t][:, c, :], ADD)
+
+        def place(t, y_rinv):
+            chunk_offsets = offsets[:, t * (CHUNK // 16):(t + 1) * (CHUNK // 16)]
+            for c in range(CB):
+                y_gained = work.tile([P, CHUNK], F32, name="y_gained", bufs=2 * CB)
+                nc.scalar.activation(y_gained[:], resid[t][:, c, :], ACT.Identity, scale=gain_f_sb[:, c:c + 1])
+                nc.vector.tensor_tensor(window[c][:].indirect(chunk_offsets), y_gained[:], y_rinv[:], MULT)
 
         first_norm(0)
-        normed = None
-        for piece in range(PIECES):
-            chunks = range(piece * CHUNKS_PER_PIECE, (piece + 1) * CHUNKS_PER_PIECE)
+        a_sb = gate_up(0)
+        first_norm(1)
+        y_rinv = {}
+        for t in range(CHUNKS):
+            down(t, a_sb)
+            y_rinv[t] = work.tile([P, CHUNK], F32, name="y_rinv", bufs=3)
+            inverse_rms(resid[t], y_rinv[t])
+            if t + 2 < CHUNKS:
+                first_norm(t + 2)
+            if t >= 1:
+                place(t - 1, y_rinv[t - 1])
+            if t + 1 < CHUNKS:
+                a_sb = gate_up(t + 1)
 
-            a_sb = {}
-            for t in chunks:
-                a_sb[t] = work.tile([P, MB, CHUNK], BF16, name="a_sb")
-                for m in range(MB):
-                    hidden = slice(m * P, (m + 1) * P)
-                    gate_ps = banks.tile([P, CHUNK], F32, name="gate_ps", tag="bank")
-                    for c in range(CB):
-                        nc.tensor.matmul(gate_ps[:], w_gate_sb[:, c, hidden], h_sb[t][:, c, :],
-                                         start=(c == 0), stop=(c == CB - 1))
-                    up_ps = banks.tile([P, CHUNK], F32, name="up_ps", tag="bank")
-                    for c in range(CB):
-                        nc.tensor.matmul(up_ps[:], w_up_sb[:, c, hidden], h_sb[t][:, c, :],
-                                         start=(c == 0), stop=(c == CB - 1))
-                    gate_silu = evacuated.tile([P, CHUNK], F32, name="gate_silu")
-                    nc.scalar.activation(gate_silu[:], gate_ps[:], ACT.Silu)
-                    up_sb = evacuated.tile([P, CHUNK], F32, name="up_sb")
-                    nc.scalar.activation(up_sb[:], up_ps[:], ACT.Copy)
-                    nc.vector.tensor_tensor(a_sb[t][:, m, :], gate_silu[:], up_sb[:], MULT)
-
-            if normed is not None:
-                place(*normed)
-            if piece + 1 < PIECES:
-                first_norm(piece + 1)
-
-            y_rinv = work.tile([P, PIECE], F32, name="y_rinv")
-            for t in chunks:
-                tokens = slice((t - chunks[0]) * CHUNK, (t - chunks[0] + 1) * CHUNK)
-                for c in range(CB):
-                    channels = slice(c * P, (c + 1) * P)
-                    down_ps = banks.tile([P, CHUNK], F32, name="down_ps", tag="bank")
-                    for m in range(MB):
-                        nc.tensor.matmul(down_ps[:], w_down_sb[:, m, channels], a_sb[t][:, m, :],
-                                         start=(m == 0), stop=(m == MB - 1))
-                    nc.vector.tensor_tensor(resid[t][:, c, :], down_ps[:], resid[t][:, c, :], ADD)
-                nc.scalar.activation(y_rinv[:, tokens], mean_of_squares(resid[t])[:], ACT.Abs_reciprocal_sqrt,
-                                     bias=eps[:], scale=1.0)
-            normed = (piece, y_rinv)
-
-        place(*normed)
+        place(CHUNKS - 1, y_rinv[CHUNKS - 1])
         for c in range(CB):
             nc.sync.dma_start(out[c * P:(c + 1) * P, :], window[c][:])

@@ -14,6 +14,7 @@ CB = C // P
 MB = M // P
 CHUNK = 512
 CHUNKS = N // CHUNK
+FIRST_HIDDEN = 2 * P
 
 FLOPS = 2 * N * 3 * C * M
 
@@ -28,7 +29,8 @@ def tile_metajanusrrpram_b_kernel(tc, base, x, gain_h, w_gate, w_up, w_down, gai
     ):
         x_blocks = x.rearrange("(b p) n -> p b n", p=P)
         resid = [held.tile([P, CB, CHUNK], F32, name=f"resid{t}") for t in range(CHUNKS)]
-        nc.sync.dma_start(resid[0][:], x_blocks[:, :, 0:CHUNK])
+        for c in range(CB):
+            nc.sync.dma_start(resid[0][:, c, :], x_blocks[:, c, 0:CHUNK])
 
         gain_h_sb = held.tile([P, CB], F32, name="gain_h_sb")
         gain_f_sb = held.tile([P, CB], F32, name="gain_f_sb")
@@ -39,8 +41,11 @@ def tile_metajanusrrpram_b_kernel(tc, base, x, gain_h, w_gate, w_up, w_down, gai
         w_gate_sb = held.tile([P, CB, M], BF16, name="w_gate_sb")
         w_up_sb = held.tile([P, CB, M], BF16, name="w_up_sb")
         w_down_sb = held.tile([P, MB, C], BF16, name="w_down_sb")
-        nc.sync.dma_start(w_gate_sb[:], w_gate.rearrange("(b p) m -> p b m", p=P))
-        nc.sync.dma_start(w_up_sb[:], w_up.rearrange("(b p) m -> p b m", p=P))
+        w_gate_blocks = w_gate.rearrange("(b p) m -> p b m", p=P)
+        w_up_blocks = w_up.rearrange("(b p) m -> p b m", p=P)
+        for hidden in (slice(0, FIRST_HIDDEN), slice(FIRST_HIDDEN, M)):
+            nc.sync.dma_start(w_gate_sb[:, :, hidden], w_gate_blocks[:, :, hidden])
+            nc.sync.dma_start(w_up_sb[:, :, hidden], w_up_blocks[:, :, hidden])
         nc.sync.dma_start(resid[1][:], x_blocks[:, :, CHUNK:2 * CHUNK])
         nc.sync.dma_start(w_down_sb[:], w_down.rearrange("(b p) c -> p b c", p=P))
         offsets = held.tile([P, N // 16], U16, name="offsets")
@@ -57,23 +62,33 @@ def tile_metajanusrrpram_b_kernel(tc, base, x, gain_h, w_gate, w_up, w_down, gai
         eps = held.tile([P, 1], F32, name="eps")
         nc.vector.memset(eps[:], EPS)
 
-        def inverse_rms(values, rinv):
-            squares = work.tile([P, CB, CHUNK], BF16, name="squares", bufs=3)
+        def inverse_rms(values, rinv, spare_tensor):
+            if spare_tensor:
+                squares = work.tile([P, CB, CHUNK], F32, name="wide_squares")
+            else:
+                squares = work.tile([P, CB, CHUNK], BF16, name="squares")
             for c in range(CB):
                 if c % 2 == 0:
                     nc.scalar.activation(squares[:, c, :], values[:, c, :], ACT.Square)
                 else:
                     nc.vector.tensor_tensor(squares[:, c, :], values[:, c, :], values[:, c, :], MULT)
             mean_ps = banks.tile([P, CHUNK], F32, name="mean_ps", tag="bank")
-            for c in range(CB):
-                nc.tensor.matmul(mean_ps[:], mean_w[:], squares[:, c, :], start=(c == 0), stop=(c == CB - 1))
+            if spare_tensor:
+                half = CB // 2
+                nc.vector.tensor_tensor(squares[:, 0:half, :], squares[:, 0:half, :], squares[:, half:CB, :], ADD)
+                summed = work.tile([P, CHUNK], BF16, name="summed")
+                nc.vector.tensor_tensor(summed[:], squares[:, 0, :], squares[:, 1, :], ADD)
+                nc.tensor.matmul(mean_ps[:], mean_w[:], summed[:], start=True, stop=True)
+            else:
+                for c in range(CB):
+                    nc.tensor.matmul(mean_ps[:], mean_w[:], squares[:, c, :], start=(c == 0), stop=(c == CB - 1))
             nc.scalar.activation(rinv[:], mean_ps[:], ACT.Abs_reciprocal_sqrt, bias=eps[:], scale=1.0)
 
         h_sb = [held.tile([P, CB, CHUNK], BF16, name=f"h{t}") for t in range(CHUNKS)]
 
         def first_norm(t):
             x_rinv = work.tile([P, CHUNK], F32, name="x_rinv")
-            inverse_rms(resid[t], x_rinv)
+            inverse_rms(resid[t], x_rinv, spare_tensor=(t > 0))
             for c in range(CB):
                 nc.vector.scalar_tensor_tensor(
                     h_sb[t][:, c, :], resid[t][:, c, :], gain_h_sb[:, c:c + 1], x_rinv[:], MULT, MULT
@@ -84,11 +99,10 @@ def tile_metajanusrrpram_b_kernel(tc, base, x, gain_h, w_gate, w_up, w_down, gai
             for m in range(MB):
                 hidden = slice(m * P, (m + 1) * P)
                 gate_ps = banks.tile([P, CHUNK], F32, name="gate_ps", tag="bank")
+                up_ps = banks.tile([P, CHUNK], F32, name="up_ps", tag="bank")
                 for c in range(CB):
                     nc.tensor.matmul(gate_ps[:], w_gate_sb[:, c, hidden], h_sb[t][:, c, :],
                                      start=(c == 0), stop=(c == CB - 1))
-                up_ps = banks.tile([P, CHUNK], F32, name="up_ps", tag="bank")
-                for c in range(CB):
                     nc.tensor.matmul(up_ps[:], w_up_sb[:, c, hidden], h_sb[t][:, c, :],
                                      start=(c == 0), stop=(c == CB - 1))
                 gate_silu = evacuated.tile([P, CHUNK], F32, name="gate_silu")
@@ -117,14 +131,13 @@ def tile_metajanusrrpram_b_kernel(tc, base, x, gain_h, w_gate, w_up, w_down, gai
 
         first_norm(0)
         a_sb = gate_up(0)
-        first_norm(1)
+        for t in range(1, CHUNKS):
+            first_norm(t)
         y_rinv = {}
         for t in range(CHUNKS):
             down(t, a_sb)
             y_rinv[t] = work.tile([P, CHUNK], F32, name="y_rinv", bufs=3)
-            inverse_rms(resid[t], y_rinv[t])
-            if t + 2 < CHUNKS:
-                first_norm(t + 2)
+            inverse_rms(resid[t], y_rinv[t], spare_tensor=False)
             if t >= 1:
                 place(t - 1, y_rinv[t - 1])
             if t + 1 < CHUNKS:

@@ -62,6 +62,10 @@ def tile_metajanusrrpram_b_kernel(tc, base, x, gain_h, w_gate, w_up, w_down, gai
         eps = held.tile([P, 1], F32, name="eps")
         nc.vector.memset(eps[:], EPS)
 
+        def call_root_table(after):
+            unused = work.tile([P, 1], F32, name="unused")
+            nc.scalar.activation(unused[:], after, ACT.Abs_reciprocal_sqrt, bias=eps[:], scale=0.0)
+
         def inverse_rms(values, rinv, spare_tensor):
             if spare_tensor:
                 squares = work.tile([P, CB, CHUNK], F32, name="wide_squares")
@@ -129,6 +133,7 @@ def tile_metajanusrrpram_b_kernel(tc, base, x, gain_h, w_gate, w_up, w_down, gai
                 nc.scalar.activation(y_gained[:], resid[t][:, c, :], ACT.Identity, scale=gain_f_sb[:, c:c + 1])
                 nc.vector.tensor_tensor(window[c][:].indirect(chunk_offsets), y_gained[:], y_rinv[:], MULT)
 
+        call_root_table(eps[:])
         first_norm(0)
         a_sb = gate_up(0)
         for t in range(1, CHUNKS):
@@ -136,6 +141,8 @@ def tile_metajanusrrpram_b_kernel(tc, base, x, gain_h, w_gate, w_up, w_down, gai
         y_rinv = {}
         for t in range(CHUNKS):
             down(t, a_sb)
+            if t == CHUNKS - 1:
+                call_root_table(resid[t][:, 0, 0:1])
             y_rinv[t] = work.tile([P, CHUNK], F32, name="y_rinv", bufs=3)
             inverse_rms(resid[t], y_rinv[t], spare_tensor=False)
             if t >= 1:

@@ -35,8 +35,7 @@ def tile_metajanusrrpram_b_kernel(tc, base, x, gain_h, w_gate, w_up, w_down, gai
         gain_h_sb = held.tile([P, CB], F32, name="gain_h_sb")
         gain_f_sb = held.tile([P, CB], F32, name="gain_f_sb")
         with nc.allow_non_contiguous_dma(reason="one gain to a partition, 512 elements in all"):
-            nc.scalar.dma_start(gain_h_sb[:], gain_h.rearrange("(b p) o -> p (b o)", p=P))
-            nc.scalar.dma_start(gain_f_sb[:], gain_f.rearrange("(b p) o -> p (b o)", p=P))
+            nc.sync.dma_start(gain_h_sb[:], gain_h.rearrange("(b p) o -> p (b o)", p=P))
 
         w_gate_sb = held.tile([P, CB, M], BF16, name="w_gate_sb")
         w_up_sb = held.tile([P, CB, M], BF16, name="w_up_sb")
@@ -48,6 +47,8 @@ def tile_metajanusrrpram_b_kernel(tc, base, x, gain_h, w_gate, w_up, w_down, gai
             nc.sync.dma_start(w_up_sb[:, :, hidden], w_up_blocks[:, :, hidden])
         nc.sync.dma_start(resid[1][:], x_blocks[:, :, CHUNK:2 * CHUNK])
         nc.sync.dma_start(w_down_sb[:], w_down.rearrange("(b p) c -> p b c", p=P))
+        with nc.allow_non_contiguous_dma(reason="one gain to a partition, 512 elements in all"):
+            nc.sync.dma_start(gain_f_sb[:], gain_f.rearrange("(b p) o -> p (b o)", p=P))
         offsets = held.tile([P, N // 16], U16, name="offsets")
         nc.sync.dma_start(offsets[:], offs)
         for t in range(2, CHUNKS):

@@ -14,6 +14,9 @@ CB = C // P
 MB = M // P
 CHUNK = 512
 CHUNKS = N // CHUNK
+ALL_TOKENS = slice(0, CHUNK)
+HALVES = (slice(0, CHUNK // 2), slice(CHUNK // 2, CHUNK))
+LAST_PARTS = (slice(0, 3 * CHUNK // 4), slice(3 * CHUNK // 4, CHUNK))
 FIRST_HIDDEN = 2 * P
 
 FLOPS = 2 * N * 3 * C * M
@@ -30,7 +33,7 @@ def tile_metajanusrrpram_b_kernel(tc, base, x, gain_h, w_gate, w_up, w_down, gai
         x_blocks = x.rearrange("(b p) n -> p b n", p=P)
         resid = [held.tile([P, CB, CHUNK], F32, name=f"resid{t}") for t in range(CHUNKS)]
         for c in range(CB):
-            nc.sync.dma_start(resid[0][:, c, :], x_blocks[:, c, 0:CHUNK])
+            nc.sync.dma_start(resid[0][:, c, HALVES[0]], x_blocks[:, c, HALVES[0]])
 
         gain_h_sb = held.tile([P, CB], F32, name="gain_h_sb")
         gain_f_sb = held.tile([P, CB], F32, name="gain_f_sb")
@@ -45,14 +48,15 @@ def tile_metajanusrrpram_b_kernel(tc, base, x, gain_h, w_gate, w_up, w_down, gai
         for hidden in (slice(0, FIRST_HIDDEN), slice(FIRST_HIDDEN, M)):
             nc.sync.dma_start(w_gate_sb[:, :, hidden], w_gate_blocks[:, :, hidden])
             nc.sync.dma_start(w_up_sb[:, :, hidden], w_up_blocks[:, :, hidden])
-        nc.sync.dma_start(resid[1][:], x_blocks[:, :, CHUNK:2 * CHUNK])
+            if hidden.start == 0:
+                nc.sync.dma_start(resid[0][:, :, HALVES[1]], x_blocks[:, :, HALVES[1]])
+        for t in range(1, CHUNKS):
+            nc.sync.dma_start(resid[t][:], x_blocks[:, :, t * CHUNK:(t + 1) * CHUNK])
         nc.sync.dma_start(w_down_sb[:], w_down.rearrange("(b p) c -> p b c", p=P))
         with nc.allow_non_contiguous_dma(reason="one gain to a partition, 512 elements in all"):
             nc.sync.dma_start(gain_f_sb[:], gain_f.rearrange("(b p) o -> p (b o)", p=P))
         offsets = held.tile([P, N // 16], U16, name="offsets")
         nc.sync.dma_start(offsets[:], offs)
-        for t in range(2, CHUNKS):
-            nc.sync.dma_start(resid[t][:], x_blocks[:, :, t * CHUNK:(t + 1) * CHUNK])
 
         window = [held.tile([P, S], F32, name=f"window{c}") for c in range(CB)]
         for c in range(CB):
@@ -67,89 +71,132 @@ def tile_metajanusrrpram_b_kernel(tc, base, x, gain_h, w_gate, w_up, w_down, gai
             unused = work.tile([P, 1], F32, name="unused")
             nc.scalar.activation(unused[:], after, ACT.Abs_reciprocal_sqrt, bias=eps[:], scale=0.0)
 
-        def inverse_rms(values, rinv, spare_tensor):
-            if spare_tensor:
-                squares = work.tile([P, CB, CHUNK], F32, name="wide_squares")
-            else:
-                squares = work.tile([P, CB, CHUNK], BF16, name="squares")
+        def square(squares, values, tokens):
             for c in range(CB):
                 if c % 2 == 0:
-                    nc.scalar.activation(squares[:, c, :], values[:, c, :], ACT.Square)
+                    nc.scalar.activation(squares[:, c, tokens], values[:, c, tokens], ACT.Square)
                 else:
-                    nc.vector.tensor_tensor(squares[:, c, :], values[:, c, :], values[:, c, :], MULT)
+                    nc.vector.tensor_tensor(squares[:, c, tokens], values[:, c, tokens], values[:, c, tokens], MULT)
+
+        def inverse_root_of_mean(rinv, addends, tokens):
             mean_ps = banks.tile([P, CHUNK], F32, name="mean_ps", tag="bank")
-            if spare_tensor:
-                half = CB // 2
-                nc.vector.tensor_tensor(squares[:, 0:half, :], squares[:, 0:half, :], squares[:, half:CB, :], ADD)
-                summed = work.tile([P, CHUNK], BF16, name="summed")
-                nc.vector.tensor_tensor(summed[:], squares[:, 0, :], squares[:, 1, :], ADD)
-                nc.tensor.matmul(mean_ps[:], mean_w[:], summed[:], start=True, stop=True)
-            else:
-                for c in range(CB):
-                    nc.tensor.matmul(mean_ps[:], mean_w[:], squares[:, c, :], start=(c == 0), stop=(c == CB - 1))
-            nc.scalar.activation(rinv[:], mean_ps[:], ACT.Abs_reciprocal_sqrt, bias=eps[:], scale=1.0)
+            for i, addend in enumerate(addends):
+                nc.tensor.matmul(mean_ps[:, tokens], mean_w[:], addend, start=(i == 0), stop=(i == len(addends) - 1))
+            nc.scalar.activation(rinv[:, tokens], mean_ps[:, tokens], ACT.Abs_reciprocal_sqrt, bias=eps[:], scale=1.0)
+
+        def inverse_rms(values, rinv, tokens):
+            squares = work.tile([P, CB, CHUNK], BF16, name="squares")
+            square(squares, values, tokens)
+            inverse_root_of_mean(rinv, [squares[:, c, tokens] for c in range(CB)], tokens)
+
+        def sum_of_squares(values):
+            squares = work.tile([P, CB, CHUNK], F32, name="wide_squares")
+            square(squares, values, ALL_TOKENS)
+            half = CB // 2
+            nc.vector.tensor_tensor(squares[:, 0:half, :], squares[:, 0:half, :], squares[:, half:CB, :], ADD)
+            summed = work.tile([P, CHUNK], BF16, name="summed", bufs=CHUNKS - 1)
+            nc.vector.tensor_tensor(summed[:], squares[:, 0, :], squares[:, 1, :], ADD)
+            return summed
 
         h_sb = [held.tile([P, CB, CHUNK], BF16, name=f"h{t}") for t in range(CHUNKS)]
 
-        def first_norm(t):
-            x_rinv = work.tile([P, CHUNK], F32, name="x_rinv")
-            inverse_rms(resid[t], x_rinv, spare_tensor=(t > 0))
+        x_rinv = {}
+
+        def make_h(t, tokens):
             for c in range(CB):
                 nc.vector.scalar_tensor_tensor(
-                    h_sb[t][:, c, :], resid[t][:, c, :], gain_h_sb[:, c:c + 1], x_rinv[:], MULT, MULT
+                    h_sb[t][:, c, tokens], resid[t][:, c, tokens], gain_h_sb[:, c:c + 1], x_rinv[t][:, tokens], MULT, MULT
                 )
 
-        def gate_up(t):
-            a_sb = work.tile([P, MB, CHUNK], BF16, name="a_sb")
-            for m in range(MB):
-                hidden = slice(m * P, (m + 1) * P)
+        def gate_up_sums(t, m, sums, tokens):
+            gate_ps, up_ps = sums
+            hidden = slice(m * P, (m + 1) * P)
+            for c in range(CB):
+                nc.tensor.matmul(gate_ps[:, tokens], w_gate_sb[:, c, hidden], h_sb[t][:, c, tokens],
+                                 start=(c == 0), stop=(c == CB - 1))
+                nc.tensor.matmul(up_ps[:, tokens], w_up_sb[:, c, hidden], h_sb[t][:, c, tokens],
+                                 start=(c == 0), stop=(c == CB - 1))
+
+        def gated(m, sums, a_sb):
+            gate_ps, up_ps = sums
+            gate_silu = evacuated.tile([P, CHUNK], F32, name="gate_silu")
+            nc.scalar.activation(gate_silu[:], gate_ps[:], ACT.Silu)
+            up_sb = evacuated.tile([P, CHUNK], F32, name="up_sb")
+            nc.scalar.activation(up_sb[:], up_ps[:], ACT.Copy)
+            nc.vector.tensor_tensor(a_sb[:, m, :], gate_silu[:], up_sb[:], MULT)
+
+        def gate_up(t, a_sb, hidden_blocks):
+            for m in hidden_blocks:
                 gate_ps = banks.tile([P, CHUNK], F32, name="gate_ps", tag="bank")
                 up_ps = banks.tile([P, CHUNK], F32, name="up_ps", tag="bank")
-                for c in range(CB):
-                    nc.tensor.matmul(gate_ps[:], w_gate_sb[:, c, hidden], h_sb[t][:, c, :],
-                                     start=(c == 0), stop=(c == CB - 1))
-                    nc.tensor.matmul(up_ps[:], w_up_sb[:, c, hidden], h_sb[t][:, c, :],
-                                     start=(c == 0), stop=(c == CB - 1))
-                gate_silu = evacuated.tile([P, CHUNK], F32, name="gate_silu")
-                nc.scalar.activation(gate_silu[:], gate_ps[:], ACT.Silu)
-                up_sb = evacuated.tile([P, CHUNK], F32, name="up_sb")
-                nc.scalar.activation(up_sb[:], up_ps[:], ACT.Copy)
-                nc.vector.tensor_tensor(a_sb[:, m, :], gate_silu[:], up_sb[:], MULT)
-            return a_sb
+                gate_up_sums(t, m, (gate_ps, up_ps), ALL_TOKENS)
+                gated(m, (gate_ps, up_ps), a_sb)
 
-        def down(t, a_sb):
-            for group in ((0, 1), (2,), (3,)):
-                down_ps = {c: banks.tile([P, CHUNK], F32, name="down_ps", tag="bank") for c in group}
-                for m in range(MB):
+        def down(t, a_sb, last_block_parts):
+            whole = (ALL_TOKENS,)
+            for group, parts in (((0, 1), whole), ((2,), whole), ((3,), last_block_parts)):
+                for tokens in parts:
+                    down_ps = {c: banks.tile([P, CHUNK], F32, name="down_ps", tag="bank") for c in group}
+                    for m in range(MB):
+                        for c in group:
+                            nc.tensor.matmul(down_ps[c][:, tokens], w_down_sb[:, m, c * P:(c + 1) * P],
+                                             a_sb[:, m, tokens], start=(m == 0), stop=(m == MB - 1))
                     for c in group:
-                        nc.tensor.matmul(down_ps[c][:], w_down_sb[:, m, c * P:(c + 1) * P], a_sb[:, m, :],
-                                         start=(m == 0), stop=(m == MB - 1))
-                for c in group:
-                    nc.vector.tensor_tensor(resid[t][:, c, :], down_ps[c][:], resid[t][:, c, :], ADD)
+                        nc.vector.tensor_tensor(resid[t][:, c, tokens], down_ps[c][:, tokens], resid[t][:, c, tokens], ADD)
 
         def place(t, y_rinv):
             chunk_offsets = offsets[:, t * (CHUNK // 16):(t + 1) * (CHUNK // 16)]
             for c in range(CB):
-                y_gained = work.tile([P, CHUNK], F32, name="y_gained", bufs=2 * CB)
+                y_gained = work.tile([P, CHUNK], F32, name="y_gained", bufs=2 * CB - 1)
                 nc.scalar.activation(y_gained[:], resid[t][:, c, :], ACT.Identity, scale=gain_f_sb[:, c:c + 1])
                 nc.vector.tensor_tensor(window[c][:].indirect(chunk_offsets), y_gained[:], y_rinv[:], MULT)
 
         call_root_table(eps[:])
-        first_norm(0)
-        a_sb = gate_up(0)
+        x_rinv[0] = work.tile([P, CHUNK], F32, name="x_rinv", bufs=CHUNKS - 1)
+        first_blocks = range(FIRST_HIDDEN // P)
+        first_sums = {}
+        inverse_rms(resid[0], x_rinv[0], HALVES[0])
+        make_h(0, HALVES[0])
+        for m in first_blocks:
+            gate_ps = banks.tile([P, CHUNK], F32, name="gate_ps", tag="bank")
+            up_ps = banks.tile([P, CHUNK], F32, name="up_ps", tag="bank")
+            first_sums[m] = (gate_ps, up_ps)
+            gate_up_sums(0, m, first_sums[m], HALVES[0])
+            if m == 0:
+                inverse_rms(resid[0], x_rinv[0], HALVES[1])
+        make_h(0, HALVES[1])
+        for m in first_blocks:
+            gate_up_sums(0, m, first_sums[m], HALVES[1])
+        a_sb = work.tile([P, MB, CHUNK], BF16, name="a_sb")
+        summed = {}
+        for m in first_blocks:
+            gated(m, first_sums[m], a_sb)
         for t in range(1, CHUNKS):
-            first_norm(t)
+            if t > 1:
+                gate_up(0, a_sb, range(2 * t - 2, 2 * t))
+            summed[t] = sum_of_squares(resid[t])
+        gate_up(0, a_sb, range(2 * CHUNKS - 2, MB))
+        for t in range(1, CHUNKS):
+            x_rinv[t] = work.tile([P, CHUNK], F32, name="x_rinv", bufs=CHUNKS - 1)
+            inverse_root_of_mean(x_rinv[t], [summed[t][:]], ALL_TOKENS)
+        make_h(1, ALL_TOKENS)
         y_rinv = {}
         for t in range(CHUNKS):
-            down(t, a_sb)
+            parts = (ALL_TOKENS,) if t + 1 < CHUNKS else LAST_PARTS
+            down(t, a_sb, parts)
             if t == CHUNKS - 1:
                 call_root_table(resid[t][:, 0, 0:1])
             y_rinv[t] = work.tile([P, CHUNK], F32, name="y_rinv", bufs=3)
-            inverse_rms(resid[t], y_rinv[t], spare_tensor=False)
+            for tokens in parts:
+                inverse_rms(resid[t], y_rinv[t], tokens)
+            if t == 0:
+                for later in range(2, CHUNKS):
+                    make_h(later, ALL_TOKENS)
             if t >= 1:
                 place(t - 1, y_rinv[t - 1])
             if t + 1 < CHUNKS:
-                a_sb = gate_up(t + 1)
+                a_sb = work.tile([P, MB, CHUNK], BF16, name="a_sb")
+                gate_up(t + 1, a_sb, range(MB))
 
         place(CHUNKS - 1, y_rinv[CHUNKS - 1])
         for c in range(CB):

@@ -84,10 +84,22 @@ def tile_metajanusrrpram_b_kernel(tc, base, x, gain_h, w_gate, w_up, w_down, gai
                 nc.tensor.matmul(mean_ps[:, tokens], mean_w[:], addend, start=(i == 0), stop=(i == len(addends) - 1))
             nc.scalar.activation(rinv[:, tokens], mean_ps[:, tokens], ACT.Abs_reciprocal_sqrt, bias=eps[:], scale=1.0)
 
-        def inverse_rms(values, rinv, tokens):
+        def plain_squares(values, tokens):
             squares = work.tile([P, CB, CHUNK], BF16, name="squares")
             square(squares, values, tokens)
-            inverse_root_of_mean(rinv, [squares[:, c, tokens] for c in range(CB)], tokens)
+            return [squares[:, c, tokens] for c in range(CB)]
+
+        def partly_added_squares(t, tokens):
+            squares = work.tile([P, CB, CHUNK], F32, name="wide_squares")
+            for c in range(CB - 1):
+                nc.scalar.activation(squares[:, c, tokens], resid[t][:, c, tokens], ACT.Square)
+            first_two = squares[:, 0, tokens]
+            nc.vector.tensor_tensor(first_two, first_two, squares[:, 1, tokens], ADD)
+            all_but_last = work.tile([P, CHUNK], BF16, name="all_but_last")
+            nc.vector.tensor_tensor(all_but_last[:, tokens], first_two, squares[:, 2, tokens], ADD)
+            last = work.tile([P, CHUNK], BF16, name="last")
+            nc.vector.tensor_tensor(last[:, tokens], resid[t][:, CB - 1, tokens], resid[t][:, CB - 1, tokens], MULT)
+            return [all_but_last[:, tokens], last[:, tokens]]
 
         def sum_of_squares(values):
             squares = work.tile([P, CB, CHUNK], F32, name="wide_squares")
@@ -101,6 +113,7 @@ def tile_metajanusrrpram_b_kernel(tc, base, x, gain_h, w_gate, w_up, w_down, gai
         h_sb = [held.tile([P, CB, CHUNK], BF16, name=f"h{t}") for t in range(CHUNKS)]
 
         x_rinv = {}
+        y_rinv = {}
 
         def make_h(t, tokens):
             for c in range(CB):
@@ -115,6 +128,11 @@ def tile_metajanusrrpram_b_kernel(tc, base, x, gain_h, w_gate, w_up, w_down, gai
                 nc.tensor.matmul(gate_ps[:, tokens], w_gate_sb[:, c, hidden], h_sb[t][:, c, tokens],
                                  start=(c == 0), stop=(c == CB - 1))
                 nc.tensor.matmul(up_ps[:, tokens], w_up_sb[:, c, hidden], h_sb[t][:, c, tokens],
+                                 start=(c == 0), stop=(c == CB - 1))
+
+        def one_sum(sum_ps, weights, t, m):
+            for c in range(CB):
+                nc.tensor.matmul(sum_ps[:], weights[:, c, m * P:(m + 1) * P], h_sb[t][:, c, :],
                                  start=(c == 0), stop=(c == CB - 1))
 
         def gated(m, sums, a_sb):
@@ -147,7 +165,7 @@ def tile_metajanusrrpram_b_kernel(tc, base, x, gain_h, w_gate, w_up, w_down, gai
         def place(t, y_rinv):
             chunk_offsets = offsets[:, t * (CHUNK // 16):(t + 1) * (CHUNK // 16)]
             for c in range(CB):
-                y_gained = work.tile([P, CHUNK], F32, name="y_gained", bufs=2 * CB - 1)
+                y_gained = work.tile([P, CHUNK], F32, name="y_gained", bufs=CB + 1)
                 nc.scalar.activation(y_gained[:], resid[t][:, c, :], ACT.Identity, scale=gain_f_sb[:, c:c + 1])
                 nc.vector.tensor_tensor(window[c][:].indirect(chunk_offsets), y_gained[:], y_rinv[:], MULT)
 
@@ -155,7 +173,7 @@ def tile_metajanusrrpram_b_kernel(tc, base, x, gain_h, w_gate, w_up, w_down, gai
         x_rinv[0] = work.tile([P, CHUNK], F32, name="x_rinv", bufs=CHUNKS - 1)
         first_blocks = range(FIRST_HIDDEN // P)
         first_sums = {}
-        inverse_rms(resid[0], x_rinv[0], HALVES[0])
+        inverse_root_of_mean(x_rinv[0], plain_squares(resid[0], HALVES[0]), HALVES[0])
         make_h(0, HALVES[0])
         for m in first_blocks:
             gate_ps = banks.tile([P, CHUNK], F32, name="gate_ps", tag="bank")
@@ -163,7 +181,7 @@ def tile_metajanusrrpram_b_kernel(tc, base, x, gain_h, w_gate, w_up, w_down, gai
             first_sums[m] = (gate_ps, up_ps)
             gate_up_sums(0, m, first_sums[m], HALVES[0])
             if m == 0:
-                inverse_rms(resid[0], x_rinv[0], HALVES[1])
+                inverse_root_of_mean(x_rinv[0], plain_squares(resid[0], HALVES[1]), HALVES[1])
         make_h(0, HALVES[1])
         for m in first_blocks:
             gate_up_sums(0, m, first_sums[m], HALVES[1])
@@ -180,23 +198,29 @@ def tile_metajanusrrpram_b_kernel(tc, base, x, gain_h, w_gate, w_up, w_down, gai
             x_rinv[t] = work.tile([P, CHUNK], F32, name="x_rinv", bufs=CHUNKS - 1)
             inverse_root_of_mean(x_rinv[t], [summed[t][:]], ALL_TOKENS)
         make_h(1, ALL_TOKENS)
-        y_rinv = {}
+        make_h(2, ALL_TOKENS)
         for t in range(CHUNKS):
             parts = (ALL_TOKENS,) if t + 1 < CHUNKS else LAST_PARTS
             down(t, a_sb, parts)
-            if t == CHUNKS - 1:
+            if t > 0:
                 call_root_table(resid[t][:, 0, 0:1])
             y_rinv[t] = work.tile([P, CHUNK], F32, name="y_rinv", bufs=3)
             for tokens in parts:
-                inverse_rms(resid[t], y_rinv[t], tokens)
+                addends = plain_squares(resid[t], tokens) if t == 0 else partly_added_squares(t, tokens)
+                if t + 1 < CHUNKS:
+                    a_sb = work.tile([P, MB, CHUNK], BF16, name="a_sb")
+                    gate_ps = banks.tile([P, CHUNK], F32, name="gate_ps", tag="bank")
+                    up_ps = banks.tile([P, CHUNK], F32, name="up_ps", tag="bank")
+                    one_sum(up_ps, w_up_sb, t + 1, 0)
+                inverse_root_of_mean(y_rinv[t], addends, tokens)
             if t == 0:
-                for later in range(2, CHUNKS):
-                    make_h(later, ALL_TOKENS)
+                make_h(3, ALL_TOKENS)
             if t >= 1:
                 place(t - 1, y_rinv[t - 1])
             if t + 1 < CHUNKS:
-                a_sb = work.tile([P, MB, CHUNK], BF16, name="a_sb")
-                gate_up(t + 1, a_sb, range(MB))
+                one_sum(gate_ps, w_gate_sb, t + 1, 0)
+                gated(0, (gate_ps, up_ps), a_sb)
+                gate_up(t + 1, a_sb, range(1, MB))
 
         place(CHUNKS - 1, y_rinv[CHUNKS - 1])
         for c in range(CB):

@@ -16,7 +16,7 @@ CHUNK = 512
 CHUNKS = N // CHUNK
 ALL_TOKENS = slice(0, CHUNK)
 HALVES = (slice(0, CHUNK // 2), slice(CHUNK // 2, CHUNK))
-LAST_PARTS = (slice(0, 3 * CHUNK // 4), slice(3 * CHUNK // 4, CHUNK))
+LAST_PARTS = HALVES
 FIRST_HIDDEN = 2 * P
 
 FLOPS = 2 * N * 3 * C * M

@@ -17,6 +17,7 @@ CHUNKS = N // CHUNK
 ALL_TOKENS = slice(0, CHUNK)
 HALVES = (slice(0, CHUNK // 2), slice(CHUNK // 2, CHUNK))
 LAST_PARTS = HALVES
+EARLY_BLOCKS = range(2)
 FIRST_HIDDEN = 2 * P
 
 FLOPS = 2 * N * 3 * C * M
@@ -209,18 +210,20 @@ def tile_metajanusrrpram_b_kernel(tc, base, x, gain_h, w_gate, w_up, w_down, gai
                 addends = plain_squares(resid[t], tokens) if t == 0 else partly_added_squares(t, tokens)
                 if t + 1 < CHUNKS:
                     a_sb = work.tile([P, MB, CHUNK], BF16, name="a_sb")
-                    gate_ps = banks.tile([P, CHUNK], F32, name="gate_ps", tag="bank")
-                    up_ps = banks.tile([P, CHUNK], F32, name="up_ps", tag="bank")
-                    one_sum(up_ps, w_up_sb, t + 1, 0)
+                    early_ups = {m: banks.tile([P, CHUNK], F32, name="up_ps", tag="bank") for m in EARLY_BLOCKS}
+                    for m in EARLY_BLOCKS:
+                        one_sum(early_ups[m], w_up_sb, t + 1, m)
                 inverse_root_of_mean(y_rinv[t], addends, tokens)
             if t == 0:
                 make_h(3, ALL_TOKENS)
             if t >= 1:
                 place(t - 1, y_rinv[t - 1])
             if t + 1 < CHUNKS:
-                one_sum(gate_ps, w_gate_sb, t + 1, 0)
-                gated(0, (gate_ps, up_ps), a_sb)
-                gate_up(t + 1, a_sb, range(1, MB))
+                for m in EARLY_BLOCKS:
+                    gate_ps = banks.tile([P, CHUNK], F32, name="gate_ps", tag="bank")
+                    one_sum(gate_ps, w_gate_sb, t + 1, m)
+                    gated(m, (gate_ps, early_ups[m]), a_sb)
+                gate_up(t + 1, a_sb, range(len(EARLY_BLOCKS), MB))
 
         place(CHUNKS - 1, y_rinv[CHUNKS - 1])
         for c in range(CB):

@@ -92,8 +92,9 @@ def tile_metajanusrrpram_b_kernel(tc, base, x, gain_h, w_gate, w_up, w_down, gai
 
         def partly_added_squares(t, tokens):
             squares = work.tile([P, CB, CHUNK], F32, name="wide_squares")
-            for c in range(CB - 1):
+            for c in (0, 2):
                 nc.scalar.activation(squares[:, c, tokens], resid[t][:, c, tokens], ACT.Square)
+            nc.vector.tensor_tensor(squares[:, 1, tokens], resid[t][:, 1, tokens], resid[t][:, 1, tokens], MULT)
             first_two = squares[:, 0, tokens]
             nc.vector.tensor_tensor(first_two, first_two, squares[:, 1, tokens], ADD)
             all_but_last = work.tile([P, CHUNK], BF16, name="all_but_last")

import concourse.mybir as mybir

F32 = mybir.dt.float32
BF16 = mybir.dt.bfloat16
U16 = mybir.dt.uint16
MULT = mybir.AluOpType.mult
ADD = mybir.AluOpType.add
ACT = mybir.ActivationFunctionType

P = 128
C, M, S, N = 512, 1024, 4096, 2048
EPS = 1e-5
CB = C // P
MB = M // P
CHUNK = 512
CHUNKS = N // CHUNK
ALL_TOKENS = slice(0, CHUNK)
HALVES = (slice(0, CHUNK // 2), slice(CHUNK // 2, CHUNK))
LAST_PARTS = HALVES
EARLY_BLOCKS = range(2)
FIRST_HIDDEN = 2 * P

FLOPS = 2 * N * 3 * C * M


def tile_metajanusrrpram_b_kernel(tc, base, x, gain_h, w_gate, w_up, w_down, gain_f, offs, out):
    nc = tc.nc
    with (
        tc.tile_pool(name="held", bufs=1) as held,
        tc.tile_pool(name="work", bufs=2) as work,
        tc.tile_pool(name="evacuated", bufs=8) as evacuated,
        tc.psum_pool(name="banks", bufs=8) as banks,
    ):
        x_blocks = x.rearrange("(b p) n -> p b n", p=P)
        resid = [held.tile([P, CB, CHUNK], F32, name=f"resid{t}") for t in range(CHUNKS)]
        for c in range(CB):
            nc.sync.dma_start(resid[0][:, c, HALVES[0]], x_blocks[:, c, HALVES[0]])

        gain_h_sb = held.tile([P, CB], F32, name="gain_h_sb")
        gain_f_sb = held.tile([P, CB], F32, name="gain_f_sb")
        with nc.allow_non_contiguous_dma(reason="one gain to a partition, 512 elements in all"):
            nc.sync.dma_start(gain_h_sb[:], gain_h.rearrange("(b p) o -> p (b o)", p=P))

        w_gate_sb = held.tile([P, CB, M], BF16, name="w_gate_sb")
        w_up_sb = held.tile([P, CB, M], BF16, name="w_up_sb")
        w_down_sb = held.tile([P, MB, C], BF16, name="w_down_sb")
        w_gate_blocks = w_gate.rearrange("(b p) m -> p b m", p=P)
        w_up_blocks = w_up.rearrange("(b p) m -> p b m", p=P)
        for hidden in (slice(0, FIRST_HIDDEN), slice(FIRST_HIDDEN, M)):
            nc.sync.dma_start(w_gate_sb[:, :, hidden], w_gate_blocks[:, :, hidden])
            nc.sync.dma_start(w_up_sb[:, :, hidden], w_up_blocks[:, :, hidden])
            if hidden.start == 0:
                nc.sync.dma_start(resid[0][:, :, HALVES[1]], x_blocks[:, :, HALVES[1]])
        for t in range(1, CHUNKS):
            nc.sync.dma_start(resid[t][:], x_blocks[:, :, t * CHUNK:(t + 1) * CHUNK])
        nc.sync.dma_start(w_down_sb[:], w_down.rearrange("(b p) c -> p b c", p=P))
        with nc.allow_non_contiguous_dma(reason="one gain to a partition, 512 elements in all"):
            nc.sync.dma_start(gain_f_sb[:], gain_f.rearrange("(b p) o -> p (b o)", p=P))
        offsets = held.tile([P, N // 16], U16, name="offsets")
        nc.sync.dma_start(offsets[:], offs)

        window = [held.tile([P, S], F32, name=f"window{c}") for c in range(CB)]
        for c in range(CB):
            nc.sync.dma_start(window[c][:], base[c * P:(c + 1) * P, :])

        mean_w = held.tile([P, P], BF16, name="mean_w")
        nc.vector.memset(mean_w[:], 1.0 / C)
        eps = held.tile([P, 1], F32, name="eps")
        nc.vector.memset(eps[:], EPS)

        def call_root_table(after):
            unused = work.tile([P, 1], F32, name="unused")
            nc.scalar.activation(unused[:], after, ACT.Abs_reciprocal_sqrt, bias=eps[:], scale=0.0)

        def square(squares, values, tokens):
            for c in range(CB):
                if c % 2 == 0:
                    nc.scalar.activation(squares[:, c, tokens], values[:, c, tokens], ACT.Square)
                else:
                    nc.vector.tensor_tensor(squares[:, c, tokens], values[:, c, tokens], values[:, c, tokens], MULT)

        def inverse_root_of_mean(rinv, addends, tokens):
            mean_ps = banks.tile([P, CHUNK], F32, name="mean_ps", tag="bank")
            for i, addend in enumerate(addends):
                nc.tensor.matmul(mean_ps[:, tokens], mean_w[:], addend, start=(i == 0), stop=(i == len(addends) - 1))
            nc.scalar.activation(rinv[:, tokens], mean_ps[:, tokens], ACT.Abs_reciprocal_sqrt, bias=eps[:], scale=1.0)

        def plain_squares(values, tokens):
            squares = work.tile([P, CB, CHUNK], BF16, name="squares")
            square(squares, values, tokens)
            return [squares[:, c, tokens] for c in range(CB)]

        def partly_added_squares(t, tokens):
            squares = work.tile([P, CB, CHUNK], F32, name="wide_squares")
            for c in (0, 2):
                nc.scalar.activation(squares[:, c, tokens], resid[t][:, c, tokens], ACT.Square)
            nc.vector.tensor_tensor(squares[:, 1, tokens], resid[t][:, 1, tokens], resid[t][:, 1, tokens], MULT)
            first_two = squares[:, 0, tokens]
            nc.vector.tensor_tensor(first_two, first_two, squares[:, 1, tokens], ADD)
            all_but_last = work.tile([P, CHUNK], BF16, name="all_but_last")
            nc.vector.tensor_tensor(all_but_last[:, tokens], first_two, squares[:, 2, tokens], ADD)
            last = work.tile([P, CHUNK], BF16, name="last")
            nc.vector.tensor_tensor(last[:, tokens], resid[t][:, CB - 1, tokens], resid[t][:, CB - 1, tokens], MULT)
            return [all_but_last[:, tokens], last[:, tokens]]

        def sum_of_squares(values):
            squares = work.tile([P, CB, CHUNK], F32, name="wide_squares")
            square(squares, values, ALL_TOKENS)
            half = CB // 2
            nc.vector.tensor_tensor(squares[:, 0:half, :], squares[:, 0:half, :], squares[:, half:CB, :], ADD)
            summed = work.tile([P, CHUNK], BF16, name="summed", bufs=CHUNKS - 1)
            nc.vector.tensor_tensor(summed[:], squares[:, 0, :], squares[:, 1, :], ADD)
            return summed

        h_sb = [held.tile([P, CB, CHUNK], BF16, name=f"h{t}") for t in range(CHUNKS)]

        x_rinv = {}
        y_rinv = {}

        def make_h(t, tokens):
            for c in range(CB):
                nc.vector.scalar_tensor_tensor(
                    h_sb[t][:, c, tokens], resid[t][:, c, tokens], gain_h_sb[:, c:c + 1], x_rinv[t][:, tokens], MULT, MULT
                )

        def gate_up_sums(t, m, sums, tokens):
            gate_ps, up_ps = sums
            hidden = slice(m * P, (m + 1) * P)
            for c in range(CB):
                nc.tensor.matmul(gate_ps[:, tokens], w_gate_sb[:, c, hidden], h_sb[t][:, c, tokens],
                                 start=(c == 0), stop=(c == CB - 1))
                nc.tensor.matmul(up_ps[:, tokens], w_up_sb[:, c, hidden], h_sb[t][:, c, tokens],
                                 start=(c == 0), stop=(c == CB - 1))

        def one_sum(sum_ps, weights, t, m):
            for c in range(CB):
                nc.tensor.matmul(sum_ps[:], weights[:, c, m * P:(m + 1) * P], h_sb[t][:, c, :],
                                 start=(c == 0), stop=(c == CB - 1))

        def gated(m, sums, a_sb):
            gate_ps, up_ps = sums
            gate_silu = evacuated.tile([P, CHUNK], F32, name="gate_silu")
            nc.scalar.activation(gate_silu[:], gate_ps[:], ACT.Silu)
            up_sb = evacuated.tile([P, CHUNK], F32, name="up_sb")
            nc.scalar.activation(up_sb[:], up_ps[:], ACT.Copy)
            nc.vector.tensor_tensor(a_sb[:, m, :], gate_silu[:], up_sb[:], MULT)

        def gate_up(t, a_sb, hidden_blocks):
            for m in hidden_blocks:
                gate_ps = banks.tile([P, CHUNK], F32, name="gate_ps", tag="bank")
                up_ps = banks.tile([P, CHUNK], F32, name="up_ps", tag="bank")
                gate_up_sums(t, m, (gate_ps, up_ps), ALL_TOKENS)
                gated(m, (gate_ps, up_ps), a_sb)

        def down(t, a_sb, last_block_parts):
            whole = (ALL_TOKENS,)
            for group, parts in (((0, 1), whole), ((2,), whole), ((3,), last_block_parts)):
                for tokens in parts:
                    down_ps = {c: banks.tile([P, CHUNK], F32, name="down_ps", tag="bank") for c in group}
                    for m in range(MB):
                        for c in group:
                            nc.tensor.matmul(down_ps[c][:, tokens], w_down_sb[:, m, c * P:(c + 1) * P],
                                             a_sb[:, m, tokens], start=(m == 0), stop=(m == MB - 1))
                    for c in group:
                        nc.vector.tensor_tensor(resid[t][:, c, tokens], down_ps[c][:, tokens], resid[t][:, c, tokens], ADD)

        def place(t, y_rinv):
            chunk_offsets = offsets[:, t * (CHUNK // 16):(t + 1) * (CHUNK // 16)]
            for c in range(CB):
                y_gained = work.tile([P, CHUNK], F32, name="y_gained", bufs=CB + 1)
                nc.scalar.activation(y_gained[:], resid[t][:, c, :], ACT.Identity, scale=gain_f_sb[:, c:c + 1])
                nc.vector.tensor_tensor(window[c][:].indirect(chunk_offsets), y_gained[:], y_rinv[:], MULT)

        call_root_table(eps[:])
        x_rinv[0] = work.tile([P, CHUNK], F32, name="x_rinv", bufs=CHUNKS - 1)
        first_blocks = range(FIRST_HIDDEN // P)
        first_sums = {}
        inverse_root_of_mean(x_rinv[0], plain_squares(resid[0], HALVES[0]), HALVES[0])
        make_h(0, HALVES[0])
        for m in first_blocks:
            gate_ps = banks.tile([P, CHUNK], F32, name="gate_ps", tag="bank")
            up_ps = banks.tile([P, CHUNK], F32, name="up_ps", tag="bank")
            first_sums[m] = (gate_ps, up_ps)
            gate_up_sums(0, m, first_sums[m], HALVES[0])
            if m == 0:
                inverse_root_of_mean(x_rinv[0], plain_squares(resid[0], HALVES[1]), HALVES[1])
        make_h(0, HALVES[1])
        for m in first_blocks:
            gate_up_sums(0, m, first_sums[m], HALVES[1])
        a_sb = work.tile([P, MB, CHUNK], BF16, name="a_sb")
        summed = {}
        for m in first_blocks:
            gated(m, first_sums[m], a_sb)
        for t in range(1, CHUNKS):
            if t > 1:
                gate_up(0, a_sb, range(2 * t - 2, 2 * t))
            summed[t] = sum_of_squares(resid[t])
        gate_up(0, a_sb, range(2 * CHUNKS - 2, MB))
        for t in range(1, CHUNKS):
            x_rinv[t] = work.tile([P, CHUNK], F32, name="x_rinv", bufs=CHUNKS - 1)
            inverse_root_of_mean(x_rinv[t], [summed[t][:]], ALL_TOKENS)
        make_h(1, ALL_TOKENS)
        make_h(2, ALL_TOKENS)
        for t in range(CHUNKS):
            parts = (ALL_TOKENS,) if t + 1 < CHUNKS else LAST_PARTS
            down(t, a_sb, parts)
            if t > 0:
                call_root_table(resid[t][:, 0, 0:1])
            y_rinv[t] = work.tile([P, CHUNK], F32, name="y_rinv", bufs=3)
            for tokens in parts:
                addends = plain_squares(resid[t], tokens) if t == 0 else partly_added_squares(t, tokens)
                if t + 1 < CHUNKS:
                    a_sb = work.tile([P, MB, CHUNK], BF16, name="a_sb")
                    early_ups = {m: banks.tile([P, CHUNK], F32, name="up_ps", tag="bank") for m in EARLY_BLOCKS}
                    for m in EARLY_BLOCKS:
                        one_sum(early_ups[m], w_up_sb, t + 1, m)
                inverse_root_of_mean(y_rinv[t], addends, tokens)
            if t == 0:
                make_h(3, ALL_TOKENS)
            if t >= 1:
                place(t - 1, y_rinv[t - 1])
            if t + 1 < CHUNKS:
                for m in EARLY_BLOCKS:
                    gate_ps = banks.tile([P, CHUNK], F32, name="gate_ps", tag="bank")
                    one_sum(gate_ps, w_gate_sb, t + 1, m)
                    gated(m, (gate_ps, early_ups[m]), a_sb)
                gate_up(t + 1, a_sb, range(len(EARLY_BLOCKS), MB))

        place(CHUNKS - 1, y_rinv[CHUNKS - 1])
        for c in range(CB):
            nc.sync.dma_start(out[c * P:(c + 1) * P, :], window[c][:])
